import numpy as np
import ml_dtypes


def mxq(x, axis, fmt="e4m3"):
    dtype, down = {"e4m3": (ml_dtypes.float8_e4m3fn, 7), "e5m2": (ml_dtypes.float8_e5m2, 14)}[fmt]
    v = np.moveaxis(np.asarray(x, np.float32).astype(ml_dtypes.bfloat16).astype(np.float64), axis, -1)
    blocks = v.reshape(v.shape[:-1] + (-1, 32))
    amax = np.abs(blocks).max(-1, keepdims=True)
    byte = np.maximum(np.where(amax > 0, np.frexp(amax)[1] - 1 + 127, 0) - down, 1)
    scale = np.exp2(byte - 127.0)
    codes = (blocks / scale).astype(np.float32).astype(dtype).astype(np.float64)
    return np.moveaxis((codes * scale).reshape(v.shape), -1, axis)


WIDE = False


def mx_kscale(k):
    if not WIDE:
        return np.ones(k)
    levels = np.array([10, -10, 5, -5, 0])
    a = np.random.permutation(np.resize(levels, k // 512 * 4)).reshape(k // 512, 4)
    idx = np.arange(k)
    return np.exp2(a[idx // 512, idx % 128 // 32])


BF16 = ml_dtypes.bfloat16


def bf(x):
    return np.asarray(x, np.float32).astype(BF16)


def f64(x):
    return np.asarray(x).astype(np.float64)


E2M1 = np.array([0.0, 0.5, 1.0, 1.5, 2.0, 3.0, 4.0, 6.0, -0.0, -0.5, -1.0, -1.5, -2.0, -3.0, -4.0, -6.0])


def pack_weight(w, fmt):
    k, n = w.shape
    w = f64(bf(w)).reshape(k // 32, 32, n)
    amax = np.abs(w).max(1)
    if fmt == "e4m3":
        byte = np.frexp(amax)[1] - 1 + 127 - 7
    else:
        mant, ex = np.frexp(amax / 6.0)
        byte = np.where(mant > 0.5, ex, ex - 1) + 127
    byte = np.clip(np.where(amax > 0, byte, 1), 1, 254)
    scaled = (w * np.exp2(127.0 - byte)[:, None, :]).reshape(k, n).astype(np.float32)
    by_word = np.ascontiguousarray(scaled.reshape(k // 512, 128, 4, n).transpose(0, 1, 3, 2))
    if fmt == "e4m3":
        words = by_word.astype(ml_dtypes.float8_e4m3fn).view(np.uint8)
    else:
        c = by_word.astype(ml_dtypes.float4_e2m1fn).view(np.uint8) & 0xF
        words = c[..., 0::2] | (c[..., 1::2] << 4)
    return np.ascontiguousarray(words), np.ascontiguousarray(byte.astype(np.uint8).reshape(k // 512, 16, n))


def unpack_weight(words, scales, fmt):
    g, p, n, _ = words.shape
    if fmt == "e4m3":
        vals = np.ascontiguousarray(words).view(ml_dtypes.float8_e4m3fn).astype(np.float64)
    else:
        nib = np.empty((g, p, n, 4), np.uint8)
        nib[..., 0::2] = words & 0xF
        nib[..., 1::2] = words >> 4
        vals = E2M1[nib]
    vals = vals * np.repeat(np.exp2(scales.astype(np.float64) - 127.0), 8, axis=1)[..., None]
    return vals.transpose(0, 1, 3, 2).reshape(g * 512, n)


B, HD, NH, H, W, F = 2, 512, 4, 32, 64, 2048
HEAD = HD // NH
P = H * W


def rms_in(x, w, eps=1e-8):
    std = np.std(x, axis=(-2, -1), keepdims=True, ddof=1)
    return x / (std + eps) * w[None, :, None, None]


def setup_inputs():
    n = np.random.standard_normal
    s = mx_kscale(HD)

    def stream():
        return n((B, NH, H, W, HEAD)) * 0.35 * (0.5 + np.random.random((B, NH, 1, 1, HEAD))) + 0.5 * n((B, NH, 1, 1, HEAD))

    xx = bf(stream())
    xy = bf(stream())
    x = bf(n((B, HD, H, W)) * (0.5 + np.random.random((B, HD, 1, 1))) + 0.5 * n((B, HD, 1, 1)))
    norm2_w = bf((1.0 + 0.1 * n(HD)) * s)
    out_w = n((HD, HD)) / np.sqrt(HD) / s[None, :]
    out_w_words, out_w_scales = pack_weight(np.ascontiguousarray(out_w.T), "e4m3")
    out_b = bf(0.1 * n(HD))
    gamma_att = bf(0.5 + 0.2 * n(HD))
    return {"xx": xx, "xy": xy,
            "x": x,
            "norm2_w": norm2_w,
            "out_w_words": out_w_words, "out_w_scales": out_w_scales,
            "out_b": out_b,
            "gamma_att": gamma_att}


def reference(xx, xy, x, norm2_w, out_w_words, out_w_scales, out_b, gamma_att):
    a = (f64(xx) + f64(xy)) * 0.5
    a = a.transpose(0, 1, 4, 2, 3).reshape(B, HD, H, W)
    a = rms_in(a, f64(norm2_w)).reshape(B, HD, P)
    a = (unpack_weight(out_w_words, out_w_scales, "e4m3").T @ mxq(a, 1, "e4m3")) + f64(out_b)[None, :, None]
    return a.reshape(B, HD, H, W) * f64(gamma_att)[None, :, None, None] + f64(x)

@@ -1,0 +1,249 @@
+from contextlib import ExitStack
+
+import concourse.mybir as mybir
+from concourse.masks import make_identity
+
+F32 = mybir.dt.float32
+BF16 = mybir.dt.bfloat16
+I32 = mybir.dt.int32
+U32 = mybir.dt.uint32
+U8 = mybir.dt.uint8
+FP8X4 = mybir.dt.float8_e4m3fn_x4
+ALU = mybir.AluOpType
+ACT = mybir.ActivationFunctionType
+AXIS = mybir.AxisListType
+
+P = 128
+PACK = 4
+BATCH = 2
+HEADS = 4
+HEAD_C = 128
+CHANNELS = HEADS * HEAD_C
+POSITIONS = 2048
+N_TILE = 512
+PARTS = POSITIONS // N_TILE
+RUN = N_TILE // P
+O_BLOCKS = CHANNELS // P
+LINE = 4
+EPS = 1e-8
+
+FLOPS = 2 * CHANNELS * CHANNELS * BATCH * POSITIONS
+
+
+def tile_axialattentionblock_pb_t_kernel(
+    tc, xx, xy, x, norm2_w, out_w_words, out_w_scales, out_b, gamma_att, out
+):
+    nc = tc.nc
+    with ExitStack() as stack:
+        consts = stack.enter_context(tc.tile_pool(name="consts", bufs=1))
+        raw_pool = stack.enter_context(tc.tile_pool(name="raw", bufs=4))
+        sum_pool = stack.enter_context(tc.tile_pool(name="sums", bufs=6))
+        turned_pool = stack.enter_context(tc.tile_pool(name="turned_sums", bufs=BATCH))
+        unread_pool = stack.enter_context(tc.tile_pool(name="unread", bufs=4))
+        stat_pool = stack.enter_context(tc.tile_pool(name="stats", bufs=2))
+        x_pool = stack.enter_context(tc.tile_pool(name="residual", bufs=BATCH))
+        mx_pool = stack.enter_context(tc.tile_pool(name="mx", bufs=3))
+        res_pool = stack.enter_context(tc.tile_pool(name="result", bufs=4))
+        turn_psum = stack.enter_context(tc.psum_pool(name="turn_psum", bufs=4))
+        acc_psum = stack.enter_context(tc.psum_pool(name="acc_psum", bufs=O_BLOCKS))
+        stack.enter_context(tc.manual_schedule())
+
+        ident = consts.tile([P, P], F32)
+        make_identity(nc, ident[:])
+
+        w_scales = consts.tile([P, CHANNELS], U8, align_bytes=64)
+        nc.vector.memset(w_scales[:].bitcast(I32), 0)
+        w_codes = consts.tile([P, CHANNELS * PACK], U8, align_bytes=64)
+
+        gamma_bf = consts.tile([P, O_BLOCKS], BF16)
+        bias_bf = consts.tile([P, O_BLOCKS], BF16)
+        with nc.allow_non_contiguous_dma(reason="two vectors of 512 values, one value to a partition"):
+            nc.scalar.dma_start(out=gamma_bf[:], in_=gamma_att.rearrange("(k p) -> p k", p=P))
+            nc.scalar.dma_start(out=bias_bf[:], in_=out_b.rearrange("(k p) -> p k", p=P))
+        norm_w = consts.tile([P, PACK], BF16)
+        nc.scalar.dma_start(out=norm_w[:], in_=norm2_w.rearrange("(q t) -> q t", t=PACK))
+
+        warm = consts.tile([P, 1], F32)
+        nc.vector.memset(warm[:], 1.0)
+        nc.scalar.activation(out=warm[:], in_=warm[:], func=ACT.Sqrt)
+
+        parts = [(b, part) for b in range(BATCH) for part in range(PARTS)]
+
+        def load_part(src, b, part, name):
+            raw = raw_pool.tile([P, HEADS, RUN, HEAD_C], BF16, name=name)
+            view = src[b].rearrange("n h w c -> n (h w) c").rearrange("n (a p r) c -> a p n (r c)", p=P, r=RUN)
+            nc.sync.dma_start(out=raw[:].rearrange("p n r c -> p n (r c)"), in_=view[part])
+            return raw
+
+        raws = {}
+        for b, part in parts:
+            raws[(b, part)] = (load_part(xx, b, part, "raw_xx"), load_part(xy, b, part, "raw_xy"))
+            if (b, part) == parts[PARTS - 1]:
+                nc.sync.dma_start(
+                    out=w_codes[:].bitcast(I32),
+                    in_=out_w_words[0].rearrange("p n t -> p (n t)").bitcast(I32),
+                )
+                for quad in range(4):
+                    nc.sync.dma_start(
+                        out=w_scales[32 * quad : 32 * quad + 4, :].bitcast(I32),
+                        in_=out_w_scales[0, 4 * quad : 4 * quad + 4, :].bitcast(I32),
+                    )
+        x_tiles = []
+        for b in range(BATCH):
+            x_sb = x_pool.tile([P, O_BLOCKS, POSITIONS], BF16, name="x_sb")
+            x_view = x[b].rearrange("(k p) h w -> k p (h w)", p=P)
+            for k in range(O_BLOCKS):
+                nc.sync.dma_start(out=x_sb[:, k, :], in_=x_view[k])
+            x_tiles.append(x_sb)
+        gamma = consts.tile([P, O_BLOCKS], F32)
+        nc.vector.tensor_copy(out=gamma[:], in_=gamma_bf[:])
+        gamma_bias = consts.tile([P, O_BLOCKS], F32)
+        nc.vector.tensor_tensor(out=gamma_bias[:], in0=gamma_bf[:], in1=bias_bf[:], op=ALU.mult)
+
+        def new_batch():
+            return {
+                "turned": turned_pool.tile([P, PACK, PARTS, RUN, P], F32, name="turned_s"),
+                "sum": stat_pool.tile([P, PACK, PARTS], F32, name="sum_parts"),
+                "square": stat_pool.tile([P, PACK, PARTS], F32, name="square_parts"),
+            }
+
+        def add_part(b, part):
+            raw_xx, raw_xy = raws[(b, part)]
+            s = sum_pool.tile([P, RUN, PACK, P], F32, name="s")
+            for t in range(PACK):
+                nc.vector.tensor_tensor(
+                    out=s[:].rearrange("p r t (n c) -> p t r n c", n=HEADS)[:, t],
+                    in0=raw_xx[:].rearrange("p n r (c t) -> p t r n c", t=PACK)[:, t],
+                    in1=raw_xy[:].rearrange("p n r (c t) -> p t r n c", t=PACK)[:, t],
+                    op=ALU.add,
+                )
+            return s
+
+        def turn_part(part, s, batch):
+            for t in range(PACK):
+                bank = turn_psum.tile([P, RUN, P], F32, name="bank")
+                for r in range(RUN):
+                    nc.tensor.transpose(bank[:, r, :], s[:, r, t, :], ident[:])
+                nc.scalar.activation(
+                    out=batch["turned"][:, t, part], in_=bank[:], func=ACT.Copy,
+                    accum_out=batch["sum"][:, t, part : part + 1],
+                )
+            for t in range(PACK):
+                unread = unread_pool.tile([P, RUN, P], BF16, name="unread")
+                nc.scalar.activation(
+                    out=unread[:], in_=batch["turned"][:, t, part], func=ACT.Square,
+                    accum_out=batch["square"][:, t, part : part + 1],
+                )
+
+        def coefficient(batch):
+            n = float(POSITIONS)
+            total = stat_pool.tile([P, PACK], F32, name="total")
+            nc.vector.tensor_reduce(out=total[:], in_=batch["sum"][:], axis=AXIS.X, op=ALU.add)
+            total_sq = stat_pool.tile([P, PACK], F32, name="total_sq")
+            nc.vector.tensor_reduce(out=total_sq[:], in_=batch["square"][:], axis=AXIS.X, op=ALU.add)
+            mean_part = stat_pool.tile([P, PACK], F32, name="mean_part")
+            nc.vector.scalar_tensor_tensor(
+                out=mean_part[:], in0=total[:], scalar=0.25 / (n * (n - 1.0)), in1=total[:],
+                op0=ALU.mult, op1=ALU.mult,
+            )
+            var = stat_pool.tile([P, PACK], F32, name="var")
+            nc.vector.scalar_tensor_tensor(
+                out=var[:], in0=total_sq[:], scalar=0.25 / (n - 1.0), in1=mean_part[:],
+                op0=ALU.mult, op1=ALU.subtract,
+            )
+            nc.vector.tensor_scalar_max(out=var[:], in0=var[:], scalar1=0.0)
+            std = stat_pool.tile([P, PACK], F32, name="std")
+            nc.scalar.activation(out=std[:], in_=var[:], func=ACT.Sqrt)
+            nc.vector.tensor_scalar_add(out=std[:], in0=std[:], scalar1=EPS)
+            inverse = stat_pool.tile([P, PACK], F32, name="inverse")
+            nc.vector.reciprocal(out=inverse[:], in_=std[:])
+            coef = stat_pool.tile([P, PACK], F32, name="coef")
+            nc.vector.scalar_tensor_tensor(
+                out=coef[:], in0=inverse[:], scalar=0.5, in1=norm_w[:], op0=ALU.mult, op1=ALU.mult
+            )
+            return coef
+
+        def residual(b, part):
+            result = res_pool.tile([P, O_BLOCKS, N_TILE], F32, name="result")
+            for k in range(O_BLOCKS):
+                x_block = x_tiles[b][:, k, part * N_TILE : (part + 1) * N_TILE]
+                if b == 0:
+                    nc.gpsimd.tensor_scalar(
+                        out=result[:, k, :], in0=x_block, scalar1=1.0, scalar2=gamma_bias[:, k : k + 1],
+                        op0=ALU.mult, op1=ALU.add,
+                    )
+                else:
+                    nc.scalar.activation(
+                        out=result[:, k, :], in_=x_block, func=ACT.Identity, bias=gamma_bias[:, k : k + 1]
+                    )
+            return result
+
+        def scale(batch, part, coef):
+            grouped = mx_pool.tile([P, N_TILE, PACK], BF16, name="grouped", align_bytes=64)
+            planes = batch["turned"][:, :, part].rearrange("q t r p -> q t (r p)")
+            nc.vector.tensor_tensor(
+                out=grouped[:].rearrange("q (c l) t -> q c t l", l=LINE),
+                in0=planes.rearrange("q t (c l) -> q c t l", l=LINE),
+                in1=coef[:].unsqueeze(1).unsqueeze(3).to_broadcast([P, N_TILE // LINE, PACK, LINE]),
+                op=ALU.mult,
+            )
+            return grouped
+
+        def quantise_and_multiply(grouped):
+            g_codes = mx_pool.tile([P, N_TILE], U32, name="g_codes", align_bytes=64)
+            g_scales = mx_pool.tile([P, N_TILE], U8, name="g_scales", align_bytes=64)
+            nc.vector.quantize_mx(
+                out=g_codes[:].bitcast(FP8X4),
+                scales=g_scales[:],
+                in_=grouped[:].rearrange("q c t -> q (c t)"),
+            )
+            products = []
+            for k in range(O_BLOCKS):
+                acc = acc_psum.tile([P, N_TILE], F32, name="acc")
+                nc.tensor.matmul_mx(
+                    out=acc[:],
+                    lhsT=w_codes[:, k * P * PACK : (k + 1) * P * PACK].bitcast(FP8X4),
+                    lhsT_scale=w_scales[:, k * P : (k + 1) * P],
+                    rhs=g_codes[:].bitcast(FP8X4),
+                    rhs_scale=g_scales[:],
+                    start=True,
+                    stop=True,
+                )
+                products.append(acc)
+            return products
+
+        def finish(b, part, products, result):
+            out_view = out[b].rearrange("(k p) h w -> k p (h w)", p=P)
+            for k in range(O_BLOCKS):
+                nc.vector.scalar_tensor_tensor(
+                    out=result[:, k, :].rearrange("o (p r) -> o p r", r=RUN),
+                    in0=products[k][:].rearrange("o (r p) -> o p r", p=P),
+                    scalar=gamma[:, k : k + 1],
+                    in1=result[:, k, :].rearrange("o (p r) -> o p r", r=RUN),
+                    op0=ALU.mult,
+                    op1=ALU.add,
+                )
+                nc.sync.dma_start(out=out_view[k][:, part * N_TILE : (part + 1) * N_TILE], in_=result[:, k, :])
+
+        batches = [new_batch() for b in range(BATCH)]
+        sums = {(b, part): add_part(b, part) for b, part in parts}
+        for b, part in parts[:PARTS]:
+            turn_part(part, sums[(b, part)], batches[b])
+
+        scaled = {}
+        multiplied = {}
+        results = {}
+        for step in range(len(parts) + 2):
+            for b, part in parts[step + PARTS : step + PARTS + 1]:
+                turn_part(part, sums[(b, part)], batches[b])
+            if 1 <= step <= len(parts):
+                multiplied[step - 1] = quantise_and_multiply(scaled[step - 1])
+            if step < len(parts):
+                b, part = parts[step]
+                if part == 0:
+                    coef = coefficient(batches[b])
+                results[step] = residual(b, part)
+                scaled[step] = scale(batches[b], part, coef)
+            if step >= 2:
+                b, part = parts[step - 2]
+                finish(b, part, multiplied[step - 2], results[step - 2])

@@ -234,14 +234,14 @@ def tile_axialattentionblock_pb_t_kernel(
         multiplied = {}
         results = {}
         for step in range(len(parts) + 2):
+            if step < len(parts) and parts[step][1] == 0:
+                coef = coefficient(batches[parts[step][0]])
             for b, part in parts[step + PARTS : step + PARTS + 1]:
                 turn_part(part, sums[(b, part)], batches[b])
             if 1 <= step <= len(parts):
                 multiplied[step - 1] = quantise_and_multiply(scaled[step - 1])
             if step < len(parts):
                 b, part = parts[step]
-                if part == 0:
-                    coef = coefficient(batches[b])
                 results[step] = residual(b, part)
                 scaled[step] = scale(batches[b], part, coef)
             if step >= 2:

@@ -26,6 +26,7 @@ RUN = N_TILE // P
 O_BLOCKS = CHANNELS // P
 LINE = 4
 EPS = 1e-8
+SCALAR_SCALES = ((1, 2), (1, 3))
 
 FLOPS = 2 * CHANNELS * CHANNELS * BATCH * POSITIONS
 
@@ -167,20 +168,21 @@ def tile_axialattentionblock_pb_t_kernel(
             result = res_pool.tile([P, O_BLOCKS, N_TILE], F32, name="result")
             for k in range(O_BLOCKS):
                 x_block = x_tiles[b][:, k, part * N_TILE : (part + 1) * N_TILE]
-                if b == 0:
-                    nc.gpsimd.tensor_scalar(
-                        out=result[:, k, :], in0=x_block, scalar1=1.0, scalar2=gamma_bias[:, k : k + 1],
-                        op0=ALU.mult, op1=ALU.add,
-                    )
-                else:
-                    nc.scalar.activation(
-                        out=result[:, k, :], in_=x_block, func=ACT.Identity, bias=gamma_bias[:, k : k + 1]
-                    )
+                nc.gpsimd.tensor_scalar(
+                    out=result[:, k, :], in0=x_block, scalar1=1.0, scalar2=gamma_bias[:, k : k + 1],
+                    op0=ALU.mult, op1=ALU.add,
+                )
             return result
 
-        def scale(batch, part, coef):
+        def scale(batch, part, coef, on_scalar):
             grouped = mx_pool.tile([P, N_TILE, PACK], BF16, name="grouped", align_bytes=64)
             planes = batch["turned"][:, :, part].rearrange("q t r p -> q t (r p)")
+            if on_scalar:
+                for t in range(PACK):
+                    nc.scalar.activation(
+                        out=grouped[:, :, t], in_=planes[:, t, :], func=ACT.Copy, scale=coef[:, t : t + 1]
+                    )
+                return grouped
             nc.vector.tensor_tensor(
                 out=grouped[:].rearrange("q (c l) t -> q c t l", l=LINE),
                 in0=planes.rearrange("q t (c l) -> q c t l", l=LINE),
@@ -243,7 +245,7 @@ def tile_axialattentionblock_pb_t_kernel(
             if step < len(parts):
                 b, part = parts[step]
                 results[step] = residual(b, part)
-                scaled[step] = scale(batches[b], part, coef)
+                scaled[step] = scale(batches[b], part, coef, (b, part) in SCALAR_SCALES)
             if step >= 2:
                 b, part = parts[step - 2]
                 finish(b, part, multiplied[step - 2], results[step - 2])

@@ -110,21 +110,26 @@ def tile_axialattentionblock_pb_t_kernel(
 
         def add_part(b, part):
             raw_xx, raw_xy = raws[(b, part)]
-            s = sum_pool.tile([P, RUN, PACK, P], F32, name="s")
-            for t in range(PACK):
-                nc.vector.tensor_tensor(
-                    out=s[:].rearrange("p r t (n c) -> p t r n c", n=HEADS)[:, t],
-                    in0=raw_xx[:].rearrange("p n r (c t) -> p t r n c", t=PACK)[:, t],
-                    in1=raw_xy[:].rearrange("p n r (c t) -> p t r n c", t=PACK)[:, t],
-                    op=ALU.add,
-                )
+            s = sum_pool.tile([P, RUN, CHANNELS], F32, name="s")
+            if (b, part) == parts[0]:
+                for t in range(PACK):
+                    nc.vector.tensor_tensor(
+                        out=s[:].rearrange("p r (n c t) -> p t r n c", n=HEADS, t=PACK)[:, t],
+                        in0=raw_xx[:].rearrange("p n r (c t) -> p t r n c", t=PACK)[:, t],
+                        in1=raw_xy[:].rearrange("p n r (c t) -> p t r n c", t=PACK)[:, t],
+                        op=ALU.add,
+                    )
+                return s
+            nc.vector.tensor_tensor(
+                out=s[:].rearrange("p r (n c) -> p n r c", n=HEADS), in0=raw_xx[:], in1=raw_xy[:], op=ALU.add
+            )
             return s
 
         def turn_part(part, s, batch):
             for t in range(PACK):
                 bank = turn_psum.tile([P, RUN, P], F32, name="bank")
                 for r in range(RUN):
-                    nc.tensor.transpose(bank[:, r, :], s[:, r, t, :], ident[:])
+                    nc.tensor.transpose(bank[:, r, :], s[:, r, :].rearrange("p (q t) -> p t q", t=PACK)[:, t], ident[:])
                 nc.scalar.activation(
                     out=batch["turned"][:, t, part], in_=bank[:], func=ACT.Copy,
                     accum_out=batch["sum"][:, t, part : part + 1],

@@ -79,7 +79,7 @@ def tile_axialattentionblock_pb_t_kernel(
         raws = {}
         for b, part in parts:
             raws[(b, part)] = (load_part(xx, b, part, "raw_xx"), load_part(xy, b, part, "raw_xy"))
-            if (b, part) == parts[PARTS - 1]:
+            if (b, part) == parts[-1]:
                 nc.sync.dma_start(
                     out=w_codes[:].bitcast(I32),
                     in_=out_w_words[0].rearrange("p n t -> p (n t)").bitcast(I32),
@@ -104,8 +104,7 @@ def tile_axialattentionblock_pb_t_kernel(
         def new_batch():
             return {
                 "turned": turned_pool.tile([P, PACK, PARTS, RUN, P], F32, name="turned_s"),
-                "sum": stat_pool.tile([P, PACK, PARTS], F32, name="sum_parts"),
-                "square": stat_pool.tile([P, PACK, PARTS], F32, name="square_parts"),
+                "stats": stat_pool.tile([P, 2, PACK, PARTS], F32, name="stats"),
             }
 
         def add_part(b, part):
@@ -114,7 +113,7 @@ def tile_axialattentionblock_pb_t_kernel(
             if (b, part) == parts[0]:
                 for t in range(PACK):
                     nc.vector.tensor_tensor(
-                        out=s[:].rearrange("p r (n c t) -> p t r n c", n=HEADS, t=PACK)[:, t],
+                        out=s[:].rearrange("p r (t n c) -> p t r n c", n=HEADS, t=PACK)[:, t],
                         in0=raw_xx[:].rearrange("p n r (c t) -> p t r n c", t=PACK)[:, t],
                         in1=raw_xy[:].rearrange("p n r (c t) -> p t r n c", t=PACK)[:, t],
                         op=ALU.add,
@@ -125,41 +124,43 @@ def tile_axialattentionblock_pb_t_kernel(
             )
             return s
 
-        def turn_part(part, s, batch):
+        def turn_part(part, s, batch, sorted_planes):
+            planes_of = "p r (t q) -> p r t q" if sorted_planes else "p r (q t) -> p r t q"
             for t in range(PACK):
                 bank = turn_psum.tile([P, RUN, P], F32, name="bank")
                 for r in range(RUN):
-                    nc.tensor.transpose(bank[:, r, :], s[:, r, :].rearrange("p (q t) -> p t q", t=PACK)[:, t], ident[:])
+                    nc.tensor.transpose(bank[:, r, :], s[:].rearrange(planes_of, t=PACK)[:, r, t], ident[:])
                 nc.scalar.activation(
                     out=batch["turned"][:, t, part], in_=bank[:], func=ACT.Copy,
-                    accum_out=batch["sum"][:, t, part : part + 1],
+                    accum_out=batch["stats"][:, 0, t, part : part + 1],
                 )
             for t in range(PACK):
                 unread = unread_pool.tile([P, RUN, P], BF16, name="unread")
                 nc.scalar.activation(
                     out=unread[:], in_=batch["turned"][:, t, part], func=ACT.Square,
-                    accum_out=batch["square"][:, t, part : part + 1],
+                    accum_out=batch["stats"][:, 1, t, part : part + 1],
                 )
 
-        def coefficient(batch):
+        def deviation(batch):
             n = float(POSITIONS)
-            total = stat_pool.tile([P, PACK], F32, name="total")
-            nc.vector.tensor_reduce(out=total[:], in_=batch["sum"][:], axis=AXIS.X, op=ALU.add)
-            total_sq = stat_pool.tile([P, PACK], F32, name="total_sq")
-            nc.vector.tensor_reduce(out=total_sq[:], in_=batch["square"][:], axis=AXIS.X, op=ALU.add)
+            totals = stat_pool.tile([P, 2, PACK], F32, name="totals")
+            nc.vector.tensor_reduce(out=totals[:], in_=batch["stats"][:], axis=AXIS.X, op=ALU.add)
             mean_part = stat_pool.tile([P, PACK], F32, name="mean_part")
             nc.vector.scalar_tensor_tensor(
-                out=mean_part[:], in0=total[:], scalar=0.25 / (n * (n - 1.0)), in1=total[:],
+                out=mean_part[:], in0=totals[:, 0], scalar=0.25 / (n * (n - 1.0)), in1=totals[:, 0],
                 op0=ALU.mult, op1=ALU.mult,
             )
             var = stat_pool.tile([P, PACK], F32, name="var")
             nc.vector.scalar_tensor_tensor(
-                out=var[:], in0=total_sq[:], scalar=0.25 / (n - 1.0), in1=mean_part[:],
+                out=var[:], in0=totals[:, 1], scalar=0.25 / (n - 1.0), in1=mean_part[:],
                 op0=ALU.mult, op1=ALU.subtract,
             )
             nc.vector.tensor_scalar_max(out=var[:], in0=var[:], scalar1=0.0)
             std = stat_pool.tile([P, PACK], F32, name="std")
             nc.scalar.activation(out=std[:], in_=var[:], func=ACT.Sqrt)
+            return std
+
+        def coefficient(std):
             nc.vector.tensor_scalar_add(out=std[:], in0=std[:], scalar1=EPS)
             inverse = stat_pool.tile([P, PACK], F32, name="inverse")
             nc.vector.reciprocal(out=inverse[:], in_=std[:])
@@ -219,9 +220,9 @@ def tile_axialattentionblock_pb_t_kernel(
                 products.append(acc)
             return products
 
-        def finish(b, part, products, result):
+        def finish(b, part, products, result, blocks):
             out_view = out[b].rearrange("(k p) h w -> k p (h w)", p=P)
-            for k in range(O_BLOCKS):
+            for k in blocks:
                 nc.vector.scalar_tensor_tensor(
                     out=result[:, k, :].rearrange("o (p r) -> o p r", r=RUN),
                     in0=products[k][:].rearrange("o (r p) -> o p r", p=P),
@@ -235,22 +236,30 @@ def tile_axialattentionblock_pb_t_kernel(
         batches = [new_batch() for b in range(BATCH)]
         sums = {(b, part): add_part(b, part) for b, part in parts}
         for b, part in parts[:PARTS]:
-            turn_part(part, sums[(b, part)], batches[b])
+            turn_part(part, sums[(b, part)], batches[b], (b, part) == parts[0])
 
         scaled = {}
         multiplied = {}
         results = {}
+        all_blocks = list(range(O_BLOCKS))
         for step in range(len(parts) + 2):
-            if step < len(parts) and parts[step][1] == 0:
-                coef = coefficient(batches[parts[step][0]])
+            new_batch_starts = step < len(parts) and parts[step][1] == 0
+            if new_batch_starts and step == 0:
+                coef = coefficient(deviation(batches[0]))
             for b, part in parts[step + PARTS : step + PARTS + 1]:
-                turn_part(part, sums[(b, part)], batches[b])
+                turn_part(part, sums[(b, part)], batches[b], (b, part) == parts[0])
             if 1 <= step <= len(parts):
                 multiplied[step - 1] = quantise_and_multiply(scaled[step - 1])
+            if new_batch_starts and step > 0:
+                b, part = parts[step - 2]
+                finish(b, part, multiplied[step - 2], results[step - 2], all_blocks[: O_BLOCKS // 2])
+                std = deviation(batches[parts[step][0]])
+                finish(b, part, multiplied[step - 2], results[step - 2], all_blocks[O_BLOCKS // 2 :])
+                coef = coefficient(std)
             if step < len(parts):
                 b, part = parts[step]
                 results[step] = residual(b, part)
                 scaled[step] = scale(batches[b], part, coef, (b, part) in SCALAR_SCALES)
-            if step >= 2:
+            if step >= 2 and not new_batch_starts:
                 b, part = parts[step - 2]
-                finish(b, part, multiplied[step - 2], results[step - 2])
+                finish(b, part, multiplied[step - 2], results[step - 2], all_blocks)

@@ -103,7 +103,7 @@ def tile_axialattentionblock_pb_t_kernel(
 
         def new_batch():
             return {
-                "turned": turned_pool.tile([P, PACK, PARTS, RUN, P], F32, name="turned_s"),
+                "turned": turned_pool.tile([P, PACK, PARTS, P, RUN], F32, name="turned_s"),
                 "stats": stat_pool.tile([P, 2, PACK, PARTS], F32, name="stats"),
             }
 
@@ -131,11 +131,11 @@ def tile_axialattentionblock_pb_t_kernel(
                 for r in range(RUN):
                     nc.tensor.transpose(bank[:, r, :], s[:].rearrange(planes_of, t=PACK)[:, r, t], ident[:])
                 nc.scalar.activation(
-                    out=batch["turned"][:, t, part], in_=bank[:], func=ACT.Copy,
+                    out=batch["turned"][:, t, part], in_=bank[:].rearrange("q r p -> q p r"), func=ACT.Copy,
                     accum_out=batch["stats"][:, 0, t, part : part + 1],
                 )
             for t in range(PACK):
-                unread = unread_pool.tile([P, RUN, P], BF16, name="unread")
+                unread = unread_pool.tile([P, P, RUN], BF16, name="unread")
                 nc.scalar.activation(
                     out=unread[:], in_=batch["turned"][:, t, part], func=ACT.Square,
                     accum_out=batch["stats"][:, 1, t, part : part + 1],
@@ -182,7 +182,7 @@ def tile_axialattentionblock_pb_t_kernel(
 
         def scale(batch, part, coef, on_scalar):
             grouped = mx_pool.tile([P, N_TILE, PACK], BF16, name="grouped", align_bytes=64)
-            planes = batch["turned"][:, :, part].rearrange("q t r p -> q t (r p)")
+            planes = batch["turned"][:, :, part].rearrange("q t p r -> q t (p r)")
             if on_scalar:
                 for t in range(PACK):
                     nc.scalar.activation(
@@ -224,10 +224,10 @@ def tile_axialattentionblock_pb_t_kernel(
             out_view = out[b].rearrange("(k p) h w -> k p (h w)", p=P)
             for k in blocks:
                 nc.vector.scalar_tensor_tensor(
-                    out=result[:, k, :].rearrange("o (p r) -> o p r", r=RUN),
-                    in0=products[k][:].rearrange("o (r p) -> o p r", p=P),
+                    out=result[:, k, :],
+                    in0=products[k][:],
                     scalar=gamma[:, k : k + 1],
-                    in1=result[:, k, :].rearrange("o (p r) -> o p r", r=RUN),
+                    in1=result[:, k, :],
                     op0=ALU.mult,
                     op1=ALU.add,
                 )

@@ -97,9 +97,7 @@ def tile_axialattentionblock_pb_t_kernel(
                 nc.sync.dma_start(out=x_sb[:, k, :], in_=x_view[k])
             x_tiles.append(x_sb)
         gamma = consts.tile([P, O_BLOCKS], F32)
-        nc.vector.tensor_copy(out=gamma[:], in_=gamma_bf[:])
         gamma_bias = consts.tile([P, O_BLOCKS], F32)
-        nc.vector.tensor_tensor(out=gamma_bias[:], in0=gamma_bf[:], in1=bias_bf[:], op=ALU.mult)
 
         def new_batch():
             return {
@@ -234,7 +232,11 @@ def tile_axialattentionblock_pb_t_kernel(
                 nc.sync.dma_start(out=out_view[k][:, part * N_TILE : (part + 1) * N_TILE], in_=result[:, k, :])
 
         batches = [new_batch() for b in range(BATCH)]
-        sums = {(b, part): add_part(b, part) for b, part in parts}
+        sums = {(b, part): add_part(b, part) for b, part in parts[:PARTS]}
+        nc.vector.tensor_copy(out=gamma[:], in_=gamma_bf[:])
+        nc.vector.tensor_tensor(out=gamma_bias[:], in0=gamma_bf[:], in1=bias_bf[:], op=ALU.mult)
+        for b, part in parts[PARTS:]:
+            sums[(b, part)] = add_part(b, part)
         for b, part in parts[:PARTS]:
             turn_part(part, sums[(b, part)], batches[b], (b, part) == parts[0])
 

@@ -56,13 +56,10 @@ def tile_axialattentionblock_pb_t_kernel(
         nc.vector.memset(w_scales[:].bitcast(I32), 0)
         w_codes = consts.tile([P, CHANNELS * PACK], U8, align_bytes=64)
 
-        gamma_bf = consts.tile([P, O_BLOCKS], BF16)
-        bias_bf = consts.tile([P, O_BLOCKS], BF16)
-        with nc.allow_non_contiguous_dma(reason="two vectors of 512 values, one value to a partition"):
-            nc.scalar.dma_start(out=gamma_bf[:], in_=gamma_att.rearrange("(k p) -> p k", p=P))
-            nc.scalar.dma_start(out=bias_bf[:], in_=out_b.rearrange("(k p) -> p k", p=P))
-        norm_w = consts.tile([P, PACK], BF16)
-        nc.scalar.dma_start(out=norm_w[:], in_=norm2_w.rearrange("(q t) -> q t", t=PACK))
+        rows = consts.tile([P, CHANNELS], BF16)
+        nc.gpsimd.memset(rows[:], 0.0)
+        ident_bf = consts.tile([P, P], BF16)
+        nc.vector.tensor_copy(out=ident_bf[:], in_=ident[:])
 
         warm = consts.tile([P, 1], F32)
         nc.vector.memset(warm[:], 1.0)
@@ -79,6 +76,9 @@ def tile_axialattentionblock_pb_t_kernel(
         raws = {}
         for b, part in parts:
             raws[(b, part)] = (load_part(xx, b, part, "raw_xx"), load_part(xy, b, part, "raw_xy"))
+            if (b, part) == parts[0]:
+                for row, vector in enumerate((gamma_att, out_b, norm2_w)):
+                    nc.sync.dma_start(out=rows[row : row + 1, :], in_=vector.unsqueeze(0))
             if (b, part) == parts[-1]:
                 nc.sync.dma_start(
                     out=w_codes[:].bitcast(I32),
@@ -98,6 +98,19 @@ def tile_axialattentionblock_pb_t_kernel(
             x_tiles.append(x_sb)
         gamma = consts.tile([P, O_BLOCKS], F32)
         gamma_bias = consts.tile([P, O_BLOCKS], F32)
+        norm_w = consts.tile([P, PACK], F32)
+
+        def turn_vectors():
+            columns = acc_psum.tile([P, O_BLOCKS + PACK, P], BF16, name="acc")
+            for k in range(O_BLOCKS):
+                nc.tensor.transpose(columns[:, k, :], rows[:, k * P : (k + 1) * P], ident_bf[:])
+            for t in range(PACK):
+                nc.tensor.transpose(
+                    columns[:, O_BLOCKS + t, :], rows[:].rearrange("p (q t) -> p t q", t=PACK)[:, t], ident_bf[:]
+                )
+            nc.vector.tensor_copy(out=gamma[:], in_=columns[:, :O_BLOCKS, 0])
+            nc.vector.tensor_tensor(out=gamma_bias[:], in0=gamma[:], in1=columns[:, :O_BLOCKS, 1], op=ALU.mult)
+            nc.vector.tensor_copy(out=norm_w[:], in_=columns[:, O_BLOCKS:, 2])
 
         def new_batch():
             return {
@@ -233,12 +246,12 @@ def tile_axialattentionblock_pb_t_kernel(
 
         batches = [new_batch() for b in range(BATCH)]
         sums = {(b, part): add_part(b, part) for b, part in parts[:PARTS]}
-        nc.vector.tensor_copy(out=gamma[:], in_=gamma_bf[:])
-        nc.vector.tensor_tensor(out=gamma_bias[:], in0=gamma_bf[:], in1=bias_bf[:], op=ALU.mult)
         for b, part in parts[PARTS:]:
             sums[(b, part)] = add_part(b, part)
         for b, part in parts[:PARTS]:
             turn_part(part, sums[(b, part)], batches[b], (b, part) == parts[0])
+            if part == 1:
+                turn_vectors()
 
         scaled = {}
         multiplied = {}

from contextlib import ExitStack

import concourse.mybir as mybir
from concourse.masks import make_identity

F32 = mybir.dt.float32
BF16 = mybir.dt.bfloat16
I32 = mybir.dt.int32
U32 = mybir.dt.uint32
U8 = mybir.dt.uint8
FP8X4 = mybir.dt.float8_e4m3fn_x4
ALU = mybir.AluOpType
ACT = mybir.ActivationFunctionType
AXIS = mybir.AxisListType

P = 128
PACK = 4
BATCH = 2
HEADS = 4
HEAD_C = 128
CHANNELS = HEADS * HEAD_C
POSITIONS = 2048
N_TILE = 512
PARTS = POSITIONS // N_TILE
RUN = N_TILE // P
O_BLOCKS = CHANNELS // P
LINE = 4
EPS = 1e-8
SCALAR_SCALES = ((1, 2), (1, 3))

FLOPS = 2 * CHANNELS * CHANNELS * BATCH * POSITIONS


def tile_axialattentionblock_pb_t_kernel(
    tc, xx, xy, x, norm2_w, out_w_words, out_w_scales, out_b, gamma_att, out
):
    nc = tc.nc
    with ExitStack() as stack:
        consts = stack.enter_context(tc.tile_pool(name="consts", bufs=1))
        raw_pool = stack.enter_context(tc.tile_pool(name="raw", bufs=4))
        sum_pool = stack.enter_context(tc.tile_pool(name="sums", bufs=6))
        turned_pool = stack.enter_context(tc.tile_pool(name="turned_sums", bufs=BATCH))
        unread_pool = stack.enter_context(tc.tile_pool(name="unread", bufs=4))
        stat_pool = stack.enter_context(tc.tile_pool(name="stats", bufs=2))
        x_pool = stack.enter_context(tc.tile_pool(name="residual", bufs=BATCH))
        mx_pool = stack.enter_context(tc.tile_pool(name="mx", bufs=3))
        res_pool = stack.enter_context(tc.tile_pool(name="result", bufs=4))
        turn_psum = stack.enter_context(tc.psum_pool(name="turn_psum", bufs=4))
        acc_psum = stack.enter_context(tc.psum_pool(name="acc_psum", bufs=O_BLOCKS))
        stack.enter_context(tc.manual_schedule())

        ident = consts.tile([P, P], F32)
        make_identity(nc, ident[:])

        w_scales = consts.tile([P, CHANNELS], U8, align_bytes=64)
        nc.vector.memset(w_scales[:].bitcast(I32), 0)
        w_codes = consts.tile([P, CHANNELS * PACK], U8, align_bytes=64)

        rows = consts.tile([P, CHANNELS], BF16)
        nc.gpsimd.memset(rows[:], 0.0)
        ident_bf = consts.tile([P, P], BF16)
        nc.vector.tensor_copy(out=ident_bf[:], in_=ident[:])

        warm = consts.tile([P, 1], F32)
        nc.vector.memset(warm[:], 1.0)
        nc.scalar.activation(out=warm[:], in_=warm[:], func=ACT.Sqrt)

        parts = [(b, part) for b in range(BATCH) for part in range(PARTS)]

        def load_part(src, b, part, name):
            raw = raw_pool.tile([P, HEADS, RUN, HEAD_C], BF16, name=name)
            view = src[b].rearrange("n h w c -> n (h w) c").rearrange("n (a p r) c -> a p n (r c)", p=P, r=RUN)
            nc.sync.dma_start(out=raw[:].rearrange("p n r c -> p n (r c)"), in_=view[part])
            return raw

        raws = {}
        for b, part in parts:
            raws[(b, part)] = (load_part(xx, b, part, "raw_xx"), load_part(xy, b, part, "raw_xy"))
            if (b, part) == parts[0]:
                for row, vector in enumerate((gamma_att, out_b, norm2_w)):
                    nc.sync.dma_start(out=rows[row : row + 1, :], in_=vector.unsqueeze(0))
            if (b, part) == parts[-1]:
                nc.sync.dma_start(
                    out=w_codes[:].bitcast(I32),
                    in_=out_w_words[0].rearrange("p n t -> p (n t)").bitcast(I32),
                )
                for quad in range(4):
                    nc.sync.dma_start(
                        out=w_scales[32 * quad : 32 * quad + 4, :].bitcast(I32),
                        in_=out_w_scales[0, 4 * quad : 4 * quad + 4, :].bitcast(I32),
                    )
        x_tiles = []
        for b in range(BATCH):
            x_sb = x_pool.tile([P, O_BLOCKS, POSITIONS], BF16, name="x_sb")
            x_view = x[b].rearrange("(k p) h w -> k p (h w)", p=P)
            for k in range(O_BLOCKS):
                nc.sync.dma_start(out=x_sb[:, k, :], in_=x_view[k])
            x_tiles.append(x_sb)
        gamma = consts.tile([P, O_BLOCKS], F32)
        gamma_bias = consts.tile([P, O_BLOCKS], F32)
        norm_w = consts.tile([P, PACK], F32)

        def turn_vectors():
            columns = acc_psum.tile([P, O_BLOCKS + PACK, P], BF16, name="acc")
            for k in range(O_BLOCKS):
                nc.tensor.transpose(columns[:, k, :], rows[:, k * P : (k + 1) * P], ident_bf[:])
            for t in range(PACK):
                nc.tensor.transpose(
                    columns[:, O_BLOCKS + t, :], rows[:].rearrange("p (q t) -> p t q", t=PACK)[:, t], ident_bf[:]
                )
            nc.vector.tensor_copy(out=gamma[:], in_=columns[:, :O_BLOCKS, 0])
            nc.vector.tensor_tensor(out=gamma_bias[:], in0=gamma[:], in1=columns[:, :O_BLOCKS, 1], op=ALU.mult)
            nc.vector.tensor_copy(out=norm_w[:], in_=columns[:, O_BLOCKS:, 2])

        def new_batch():
            return {
                "turned": turned_pool.tile([P, PACK, PARTS, P, RUN], F32, name="turned_s"),
                "stats": stat_pool.tile([P, 2, PACK, PARTS], F32, name="stats"),
            }

        def add_part(b, part):
            raw_xx, raw_xy = raws[(b, part)]
            s = sum_pool.tile([P, RUN, CHANNELS], F32, name="s")
            if (b, part) == parts[0]:
                for t in range(PACK):
                    nc.vector.tensor_tensor(
                        out=s[:].rearrange("p r (t n c) -> p t r n c", n=HEADS, t=PACK)[:, t],
                        in0=raw_xx[:].rearrange("p n r (c t) -> p t r n c", t=PACK)[:, t],
                        in1=raw_xy[:].rearrange("p n r (c t) -> p t r n c", t=PACK)[:, t],
                        op=ALU.add,
                    )
                return s
            nc.vector.tensor_tensor(
                out=s[:].rearrange("p r (n c) -> p n r c", n=HEADS), in0=raw_xx[:], in1=raw_xy[:], op=ALU.add
            )
            return s

        def turn_part(part, s, batch, sorted_planes):
            planes_of = "p r (t q) -> p r t q" if sorted_planes else "p r (q t) -> p r t q"
            for t in range(PACK):
                bank = turn_psum.tile([P, RUN, P], F32, name="bank")
                for r in range(RUN):
                    nc.tensor.transpose(bank[:, r, :], s[:].rearrange(planes_of, t=PACK)[:, r, t], ident[:])
                nc.scalar.activation(
                    out=batch["turned"][:, t, part], in_=bank[:].rearrange("q r p -> q p r"), func=ACT.Copy,
                    accum_out=batch["stats"][:, 0, t, part : part + 1],
                )
            for t in range(PACK):
                unread = unread_pool.tile([P, P, RUN], BF16, name="unread")
                nc.scalar.activation(
                    out=unread[:], in_=batch["turned"][:, t, part], func=ACT.Square,
                    accum_out=batch["stats"][:, 1, t, part : part + 1],
                )

        def deviation(batch):
            n = float(POSITIONS)
            totals = stat_pool.tile([P, 2, PACK], F32, name="totals")
            nc.vector.tensor_reduce(out=totals[:], in_=batch["stats"][:], axis=AXIS.X, op=ALU.add)
            mean_part = stat_pool.tile([P, PACK], F32, name="mean_part")
            nc.vector.scalar_tensor_tensor(
                out=mean_part[:], in0=totals[:, 0], scalar=0.25 / (n * (n - 1.0)), in1=totals[:, 0],
                op0=ALU.mult, op1=ALU.mult,
            )
            var = stat_pool.tile([P, PACK], F32, name="var")
            nc.vector.scalar_tensor_tensor(
                out=var[:], in0=totals[:, 1], scalar=0.25 / (n - 1.0), in1=mean_part[:],
                op0=ALU.mult, op1=ALU.subtract,
            )
            nc.vector.tensor_scalar_max(out=var[:], in0=var[:], scalar1=0.0)
            std = stat_pool.tile([P, PACK], F32, name="std")
            nc.scalar.activation(out=std[:], in_=var[:], func=ACT.Sqrt)
            return std

        def coefficient(std):
            nc.vector.tensor_scalar_add(out=std[:], in0=std[:], scalar1=EPS)
            inverse = stat_pool.tile([P, PACK], F32, name="inverse")
            nc.vector.reciprocal(out=inverse[:], in_=std[:])
            coef = stat_pool.tile([P, PACK], F32, name="coef")
            nc.vector.scalar_tensor_tensor(
                out=coef[:], in0=inverse[:], scalar=0.5, in1=norm_w[:], op0=ALU.mult, op1=ALU.mult
            )
            return coef

        def residual(b, part):
            result = res_pool.tile([P, O_BLOCKS, N_TILE], F32, name="result")
            for k in range(O_BLOCKS):
                x_block = x_tiles[b][:, k, part * N_TILE : (part + 1) * N_TILE]
                nc.gpsimd.tensor_scalar(
                    out=result[:, k, :], in0=x_block, scalar1=1.0, scalar2=gamma_bias[:, k : k + 1],
                    op0=ALU.mult, op1=ALU.add,
                )
            return result

        def scale(batch, part, coef, on_scalar):
            grouped = mx_pool.tile([P, N_TILE, PACK], BF16, name="grouped", align_bytes=64)
            planes = batch["turned"][:, :, part].rearrange("q t p r -> q t (p r)")
            if on_scalar:
                for t in range(PACK):
                    nc.scalar.activation(
                        out=grouped[:, :, t], in_=planes[:, t, :], func=ACT.Copy, scale=coef[:, t : t + 1]
                    )
                return grouped
            nc.vector.tensor_tensor(
                out=grouped[:].rearrange("q (c l) t -> q c t l", l=LINE),
                in0=planes.rearrange("q t (c l) -> q c t l", l=LINE),
                in1=coef[:].unsqueeze(1).unsqueeze(3).to_broadcast([P, N_TILE // LINE, PACK, LINE]),
                op=ALU.mult,
            )
            return grouped

        def quantise_and_multiply(grouped):
            g_codes = mx_pool.tile([P, N_TILE], U32, name="g_codes", align_bytes=64)
            g_scales = mx_pool.tile([P, N_TILE], U8, name="g_scales", align_bytes=64)
            nc.vector.quantize_mx(
                out=g_codes[:].bitcast(FP8X4),
                scales=g_scales[:],
                in_=grouped[:].rearrange("q c t -> q (c t)"),
            )
            products = []
            for k in range(O_BLOCKS):
                acc = acc_psum.tile([P, N_TILE], F32, name="acc")
                nc.tensor.matmul_mx(
                    out=acc[:],
                    lhsT=w_codes[:, k * P * PACK : (k + 1) * P * PACK].bitcast(FP8X4),
                    lhsT_scale=w_scales[:, k * P : (k + 1) * P],
                    rhs=g_codes[:].bitcast(FP8X4),
                    rhs_scale=g_scales[:],
                    start=True,
                    stop=True,
                )
                products.append(acc)
            return products

        def finish(b, part, products, result, blocks):
            out_view = out[b].rearrange("(k p) h w -> k p (h w)", p=P)
            for k in blocks:
                nc.vector.scalar_tensor_tensor(
                    out=result[:, k, :],
                    in0=products[k][:],
                    scalar=gamma[:, k : k + 1],
                    in1=result[:, k, :],
                    op0=ALU.mult,
                    op1=ALU.add,
                )
                nc.sync.dma_start(out=out_view[k][:, part * N_TILE : (part + 1) * N_TILE], in_=result[:, k, :])

        batches = [new_batch() for b in range(BATCH)]
        sums = {(b, part): add_part(b, part) for b, part in parts[:PARTS]}
        for b, part in parts[PARTS:]:
            sums[(b, part)] = add_part(b, part)
        for b, part in parts[:PARTS]:
            turn_part(part, sums[(b, part)], batches[b], (b, part) == parts[0])
            if part == 1:
                turn_vectors()

        scaled = {}
        multiplied = {}
        results = {}
        all_blocks = list(range(O_BLOCKS))
        for step in range(len(parts) + 2):
            new_batch_starts = step < len(parts) and parts[step][1] == 0
            if new_batch_starts and step == 0:
                coef = coefficient(deviation(batches[0]))
            for b, part in parts[step + PARTS : step + PARTS + 1]:
                turn_part(part, sums[(b, part)], batches[b], (b, part) == parts[0])
            if 1 <= step <= len(parts):
                multiplied[step - 1] = quantise_and_multiply(scaled[step - 1])
            if new_batch_starts and step > 0:
                b, part = parts[step - 2]
                finish(b, part, multiplied[step - 2], results[step - 2], all_blocks[: O_BLOCKS // 2])
                std = deviation(batches[parts[step][0]])
                finish(b, part, multiplied[step - 2], results[step - 2], all_blocks[O_BLOCKS // 2 :])
                coef = coefficient(std)
            if step < len(parts):
                b, part = parts[step]
                results[step] = residual(b, part)
                scaled[step] = scale(batches[b], part, coef, (b, part) in SCALAR_SCALES)
            if step >= 2 and not new_batch_starts:
                b, part = parts[step - 2]
                finish(b, part, multiplied[step - 2], results[step - 2], all_blocks)
